import numpy as np
import ml_dtypes


def mxq(x, axis, fmt="e4m3"):
    dtype, down = {"e4m3": (ml_dtypes.float8_e4m3fn, 7), "e5m2": (ml_dtypes.float8_e5m2, 14)}[fmt]
    v = np.moveaxis(np.asarray(x, np.float32).astype(ml_dtypes.bfloat16).astype(np.float64), axis, -1)
    blocks = v.reshape(v.shape[:-1] + (-1, 32))
    amax = np.abs(blocks).max(-1, keepdims=True)
    byte = np.maximum(np.where(amax > 0, np.frexp(amax)[1] - 1 + 127, 0) - down, 1)
    scale = np.exp2(byte - 127.0)
    codes = (blocks / scale).astype(np.float32).astype(dtype).astype(np.float64)
    return np.moveaxis((codes * scale).reshape(v.shape), -1, axis)


WIDE = False


def mx_kscale(k):
    if not WIDE:
        return np.ones(k)
    levels = np.array([10, -10, 5, -5, 0])
    if k % 512:
        return np.exp2(np.random.permutation(np.resize(levels, k // 32))).repeat(32)
    a = np.empty((k // 512, 16))
    for p in range(k // 512):
        a[p, :8] = np.random.permutation(np.resize(levels, 8))
        for g in range(8):
            far = levels[np.abs(levels - a[p, g]) >= 10]
            a[p, g + 8] = far[np.random.randint(len(far))]
    return np.exp2(a.ravel()).repeat(32)


BF16 = ml_dtypes.bfloat16


def bf(x):
    return np.asarray(x, np.float32).astype(BF16)


def f64(x):
    return np.asarray(x).astype(np.float64)


B, S, D, H, HD, F = 4, 2048, 1024, 2, 64, 4096
E = H * HD
CURV = 1.0


def lift(space):
    t = np.sqrt(np.sum(space * space, -1, keepdims=True) + 1.0 / CURV)
    return np.concatenate([t, space], -1)


def setup_inputs():
    s = mx_kscale(D)
    return {"x_space": bf(np.random.standard_normal((B, S, D)) * 2.0 / np.sqrt(D)),
            "ln1_w": bf((1.0 + 0.1 * np.random.standard_normal(D)) * s),
            "wq": bf(np.random.standard_normal((D, E)) * 0.5 / np.sqrt(D) / s[:, None]),
            "wk": bf(np.random.standard_normal((D, E)) * 0.5 / np.sqrt(D) / s[:, None]),
            "wv": bf(np.random.standard_normal((D, E)) * 0.25 / np.sqrt(D) / s[:, None])}


def reference(x_space, ln1_w, wq, wk, wv):
    s = f64(x_space)
    rms = np.sqrt(np.mean(s * s, -1, keepdims=True) + 1e-6)
    nq = mxq(s / rms * f64(ln1_w), 2, "e4m3")
    q = lift((nq @ mxq(f64(wq), 0, "e4m3")).reshape(B, S, H, HD))
    k = lift((nq @ mxq(f64(wk), 0, "e4m3")).reshape(B, S, H, HD))
    v = lift((nq @ mxq(f64(wv), 0, "e4m3")).reshape(B, S, H, HD))
    return q, k, v

@@ -1,0 +1,248 @@
+from contextlib import ExitStack
+
+import concourse.mybir as mybir
+from concourse.masks import make_identity
+
+FLOPS = 2 * 4 * 2048 * 1024 * 384
+
+F32 = mybir.dt.float32
+BF16 = mybir.dt.bfloat16
+U32 = mybir.dt.uint32
+U8 = mybir.dt.uint8
+FP8X4 = mybir.dt.float8_e4m3fn_x4
+ACT = mybir.ActivationFunctionType
+ALU = mybir.AluOpType
+
+P = 128
+PACK = 4
+K_PASS = P * PACK
+D = 1024
+PASSES = D // K_PASS
+TOKENS = 4 * 2048
+TILES = 4
+GROUP = TILES * P
+GROUPS = TOKENS // GROUP
+UNITS = GROUPS * TILES
+HEADS = 2
+HD = 64
+E = HEADS * HD
+OUTS = 3
+QK = 2 * E
+EPS = 1e-6
+
+SUM_LEAD = 8
+SCALE_LEAD = 3
+TURN_LEAD = 1
+QUANT_LAG = 1
+PROJECT_LAG = 2
+LIFT_LAG = 3
+HEAD_SUM_LAG = 4
+STORE_LAG = 5
+LOAD_AHEAD = 2
+
+
+def quantise_weights(nc, const, stage, wq, wk, wv):
+    raw = stage.tile([P, PASSES, PACK, OUTS * E], BF16)
+    for o, w in enumerate((wq, wk, wv)):
+        for g in range(PASSES):
+            nc.sync.dma_start(
+                out=raw[:, g, :, o * E : (o + 1) * E],
+                in_=w[g * K_PASS : (g + 1) * K_PASS, :].rearrange("(p t) n -> p t n", t=PACK),
+            )
+    operands = []
+    for name, first, cols in (("qk", 0, QK), ("v", QK, E)):
+        grouped = stage.tile([P, PASSES, cols, PACK], BF16, name="w_grouped_" + name, align_bytes=64)
+        for g in range(PASSES):
+            nc.vector.tensor_copy(
+                out=grouped[:, g, :, :],
+                in_=raw[:, g, :, first : first + cols].rearrange("p t c -> p c t"),
+            )
+        codes = const.tile([P, PASSES, cols], U32, name="w_codes_" + name, align_bytes=64)
+        scales = const.tile([P, PASSES, cols], U8, name="w_scales_" + name, align_bytes=64)
+        operands.append((first, cols, grouped, codes, scales))
+    for first, cols, grouped, codes, scales in operands:
+        nc.vector.quantize_mx(
+            out=codes[:].rearrange("p g c -> p (g c)").bitcast(FP8X4),
+            scales=scales[:].rearrange("p g c -> p (g c)"),
+            in_=grouped[:].rearrange("p g c t -> p (g c t)"),
+        )
+    return [(first, cols, codes, scales) for first, cols, grouped, codes, scales in operands]
+
+
+def gain_by_partition(nc, const, ln1_w):
+    raw = const.tile([P, PASSES, PACK], BF16, name="gain_raw")
+    nc.sync.dma_start(out=raw[:], in_=ln1_w.rearrange("(g p t) -> p g t", g=PASSES, t=PACK))
+    gain = const.tile([P, PASSES, PACK], F32)
+    nc.vector.tensor_copy(out=gain[:], in_=raw[:])
+    return gain
+
+
+def tile_ltransformerdecoderblock_pa_t_kernel(
+    tc, x_space, ln1_w, wq, wk, wv, out_0, out_1, out_2
+):
+    nc = tc.nc
+    x_rows = x_space.rearrange("b s d -> (b s) d")
+    out_rows = [o.rearrange("b s h c -> (b s) (h c)") for o in (out_0, out_1, out_2)]
+
+    with ExitStack() as ctx:
+        const = ctx.enter_context(tc.tile_pool(name="const", bufs=1))
+        stage = ctx.enter_context(tc.tile_pool(name="stage", bufs=1))
+        x_pool = ctx.enter_context(tc.tile_pool(name="x", bufs=LOAD_AHEAD + 3))
+        by_group = ctx.enter_context(tc.tile_pool(name="by_group", bufs=4))
+        by_unit = ctx.enter_context(tc.tile_pool(name="by_unit", bufs=4))
+        psum_t = ctx.enter_context(tc.psum_pool(name="psum_t", bufs=4))
+        psum_o = ctx.enter_context(tc.psum_pool(name="psum_o", bufs=4))
+        ctx.enter_context(tc.manual_schedule())
+
+        x_sb = {}
+        sum_sq = {}
+        rms = {}
+        rstd = {}
+        lifted = {}
+        head_sq = {}
+        y = {}
+        turned = {}
+        n_grouped = {}
+        n_codes = {}
+        n_scales = {}
+        product = {}
+        squared = {}
+
+        def load_group(i):
+            x_sb[i] = x_pool.tile([P, TILES, D], BF16, name="x_sb")
+            nc.sync.dma_start(
+                out=x_sb[i][:],
+                in_=x_rows[i * GROUP : (i + 1) * GROUP, :].rearrange("(p j) d -> p j d", j=TILES),
+            )
+
+        def sum_squares(u):
+            i, j = divmod(u, TILES)
+            if j == 0:
+                sum_sq[i] = by_group.tile([P, TILES], F32, name="sum_sq")
+            scratch = by_unit.tile([P, D], BF16, name="scratch")
+            nc.scalar.activation(
+                out=scratch[:], in_=x_sb[i][:, j, :], func=ACT.Square,
+                accum_out=sum_sq[i][:, j : j + 1],
+            )
+            if j == TILES - 1:
+                rms[i] = by_group.tile([P, TILES], F32, name="rms")
+                nc.scalar.activation(
+                    out=rms[i][:], in_=sum_sq[i][:], func=ACT.Sqrt, scale=1.0 / D, bias=EPS
+                )
+
+        def invert_rms(i):
+            rstd[i] = by_group.tile([P, TILES], F32, name="rstd")
+            nc.vector.reciprocal(out=rstd[i][:], in_=rms[i][:])
+
+        def scale_rows(u):
+            i, j = divmod(u, TILES)
+            y[u] = by_unit.tile([P, PASSES, PACK, P], F32, name="y")
+            nc.gpsimd.tensor_scalar(
+                out=y[u][:],
+                in0=x_sb[i][:, j, :].rearrange("r (g p t) -> r g t p", g=PASSES, t=PACK),
+                scalar1=rstd[i][:, j : j + 1], scalar2=1.0, op0=ALU.mult, op1=ALU.mult,
+            )
+
+        def turn(u):
+            for g in range(PASSES):
+                turned[u, g] = psum_t.tile([P, PACK, P], F32, name="turned")
+                for t in range(PACK):
+                    nc.tensor.transpose(turned[u, g][:, t, :], y[u][:, g, t, :], ident[:])
+
+        def apply_gain(u):
+            n_grouped[u] = by_unit.tile([P, PASSES, P, PACK], BF16, name="n_grouped", align_bytes=64)
+            for g in range(PASSES):
+                nc.vector.tensor_tensor(
+                    out=n_grouped[u][:, g, :, :],
+                    in0=turned[u, g][:].rearrange("p t r -> p r t"),
+                    in1=gain[:, g, :].unsqueeze(1).to_broadcast([P, P, PACK]),
+                    op=ALU.mult,
+                )
+
+        def quantise(u):
+            n_codes[u] = by_unit.tile([P, PASSES, P], U32, name="n_codes", align_bytes=64)
+            n_scales[u] = by_unit.tile([P, PASSES, P], U8, name="n_scales", align_bytes=64)
+            nc.vector.quantize_mx(
+                out=n_codes[u][:].rearrange("p g r -> p (g r)").bitcast(FP8X4),
+                scales=n_scales[u][:].rearrange("p g r -> p (g r)"),
+                in_=n_grouped[u][:].rearrange("p g r t -> p (g r t)"),
+            )
+
+        def project(u):
+            product[u] = psum_o.tile([P, OUTS * E], F32, name="product")
+            for first, cols, w_codes, w_scales in weights:
+                for g in range(PASSES):
+                    nc.tensor.matmul_mx(
+                        out=product[u][:, first : first + cols],
+                        lhsT=n_codes[u][:, g, :].bitcast(FP8X4),
+                        lhsT_scale=n_scales[u][:, g, :],
+                        rhs=w_codes[:, g, :].bitcast(FP8X4),
+                        rhs_scale=w_scales[:, g, :],
+                        start=(g == 0),
+                        stop=(g == PASSES - 1),
+                    )
+
+        def lift(u):
+            i, j = divmod(u, TILES)
+            if j == 0:
+                lifted[i] = by_group.tile([P, OUTS, TILES, HEADS, 1 + HD], F32, name="lifted")
+            by_head = product[u][:].rearrange("p (o h c) -> p o h c", o=OUTS, h=HEADS)
+            nc.scalar.copy(out=lifted[i][:, :, j, :, 1:], in_=by_head)
+            squared[u] = by_unit.tile([P, OUTS, HEADS, HD], F32, name="squared")
+            nc.scalar.activation(out=squared[u][:], in_=by_head, func=ACT.Square)
+
+        def sum_heads(u):
+            i, j = divmod(u, TILES)
+            if j == 0:
+                head_sq[i] = by_group.tile([P, OUTS, TILES, HEADS], F32, name="head_sq")
+            nc.vector.tensor_reduce(
+                out=head_sq[i][:, :, j, :], in_=squared[u][:], axis=mybir.AxisListType.X, op=ALU.add
+            )
+
+        def store_group(i):
+            nc.scalar.activation(
+                out=lifted[i][:, :, :, :, 0], in_=head_sq[i][:], func=ACT.Sqrt, bias=1.0
+            )
+            for o in range(OUTS):
+                nc.sync.dma_start(
+                    out=out_rows[o][i * GROUP : (i + 1) * GROUP, :].rearrange(
+                        "(p j) c -> p (j c)", j=TILES
+                    ),
+                    in_=lifted[i][:, o, :, :, :].rearrange("p j h c -> p (j h c)"),
+                )
+
+        load_group(0)
+        ident = const.tile([P, P], F32)
+        make_identity(nc, ident[:])
+        gain = gain_by_partition(nc, const, ln1_w)
+        weights = quantise_weights(nc, const, stage, wq, wk, wv)
+        for i in range(1, LOAD_AHEAD):
+            load_group(i)
+
+        def is_unit(u):
+            return 0 <= u < UNITS
+
+        for s in range(-SUM_LEAD, UNITS + STORE_LAG):
+            if is_unit(s + SUM_LEAD) and (s + SUM_LEAD) % TILES == 0:
+                if (s + SUM_LEAD) // TILES + LOAD_AHEAD < GROUPS:
+                    load_group((s + SUM_LEAD) // TILES + LOAD_AHEAD)
+            if is_unit(s - STORE_LAG) and (s - STORE_LAG) % TILES == TILES - 1:
+                store_group((s - STORE_LAG) // TILES)
+            if is_unit(s + SUM_LEAD):
+                sum_squares(s + SUM_LEAD)
+            if is_unit(s + SCALE_LEAD + 1) and (s + SCALE_LEAD + 1) % TILES == 0:
+                invert_rms((s + SCALE_LEAD + 1) // TILES)
+            if is_unit(s + SCALE_LEAD):
+                scale_rows(s + SCALE_LEAD)
+            if is_unit(s - PROJECT_LAG):
+                project(s - PROJECT_LAG)
+            if is_unit(s + TURN_LEAD):
+                turn(s + TURN_LEAD)
+            if is_unit(s):
+                apply_gain(s)
+            if is_unit(s - QUANT_LAG):
+                quantise(s - QUANT_LAG)
+            if is_unit(s - LIFT_LAG):
+                lift(s - LIFT_LAG)
+            if is_unit(s - HEAD_SUM_LAG):
+                sum_heads(s - HEAD_SUM_LAG)

@@ -1,3 +1,4 @@
+import math
 from contextlib import ExitStack
 
 import concourse.mybir as mybir
@@ -36,8 +37,9 @@ TURN_LEAD = 1
 QUANT_LAG = 1
 PROJECT_LAG = 2
 LIFT_LAG = 3
-HEAD_SUM_LAG = 4
-STORE_LAG = 5
+STATS_LAG = 4
+SUM_LAG = 5
+STORE_LAG = 6
 LOAD_AHEAD = 2
 
 
@@ -99,6 +101,7 @@ def tile_ltransformerdecoderblock_pa_t_kernel(
         rms = {}
         rstd = {}
         lifted = {}
+        stats = {}
         head_sq = {}
         y = {}
         turned = {}
@@ -106,7 +109,6 @@ def tile_ltransformerdecoderblock_pa_t_kernel(
         n_codes = {}
         n_scales = {}
         product = {}
-        squared = {}
 
         def load_group(i):
             x_sb[i] = x_pool.tile([P, TILES, D], BF16, name="x_sb")
@@ -188,15 +190,25 @@ def tile_ltransformerdecoderblock_pa_t_kernel(
                 lifted[i] = by_group.tile([P, OUTS, TILES, HEADS, 1 + HD], F32, name="lifted")
             by_head = product[u][:].rearrange("p (o h c) -> p o h c", o=OUTS, h=HEADS)
             nc.scalar.copy(out=lifted[i][:, :, j, :, 1:], in_=by_head)
-            squared[u] = by_unit.tile([P, OUTS, HEADS, HD], F32, name="squared")
-            nc.scalar.activation(out=squared[u][:], in_=by_head, func=ACT.Square)
 
-        def sum_heads(u):
+        def head_stats(u):
             i, j = divmod(u, TILES)
             if j == 0:
-                head_sq[i] = by_group.tile([P, OUTS, TILES, HEADS], F32, name="head_sq")
-            nc.vector.tensor_reduce(
-                out=head_sq[i][:, :, j, :], in_=squared[u][:], axis=mybir.AxisListType.X, op=ALU.add
+                stats[i] = by_group.tile([P, OUTS, TILES, HEADS, 3], F32, name="stats")
+            for o in range(OUTS):
+                nc.vector.bn_stats(
+                    out=stats[i][:, o, j, :, :].rearrange("p h m -> p (h m)"),
+                    in_=product[u][:, o * E : (o + 1) * E].rearrange("p (h c) -> p c h", h=HEADS),
+                )
+
+        def sum_heads(i):
+            mean_sq = by_group.tile([P, OUTS, TILES, HEADS], F32, name="mean_sq")
+            nc.scalar.activation(
+                out=mean_sq[:], in_=stats[i][:, :, :, :, 1], func=ACT.Square, scale=math.sqrt(HD)
+            )
+            head_sq[i] = by_group.tile([P, OUTS, TILES, HEADS], F32, name="head_sq")
+            nc.gpsimd.tensor_tensor(
+                out=head_sq[i][:], in0=stats[i][:, :, :, :, 2], in1=mean_sq[:], op=ALU.add
             )
 
         def store_group(i):
@@ -244,5 +256,7 @@ def tile_ltransformerdecoderblock_pa_t_kernel(
                 quantise(s - QUANT_LAG)
             if is_unit(s - LIFT_LAG):
                 lift(s - LIFT_LAG)
-            if is_unit(s - HEAD_SUM_LAG):
-                sum_heads(s - HEAD_SUM_LAG)
+            if is_unit(s - STATS_LAG):
+                head_stats(s - STATS_LAG)
+            if is_unit(s - SUM_LAG) and (s - SUM_LAG) % TILES == TILES - 1:
+                sum_heads((s - SUM_LAG) // TILES)

@@ -132,9 +132,10 @@ def tile_ltransformerdecoderblock_pa_t_kernel(
                     out=rms[i][:], in_=sum_sq[i][:], func=ACT.Sqrt, scale=1.0 / D, bias=EPS
                 )
 
-        def invert_rms(i):
-            rstd[i] = by_group.tile([P, TILES], F32, name="rstd")
-            nc.vector.reciprocal(out=rstd[i][:], in_=rms[i][:])
+        def invert_rms(u):
+            i, j = divmod(u, TILES)
+            rstd[u] = by_unit.tile([P, 1], F32, name="rstd")
+            nc.vector.reciprocal(out=rstd[u][:], in_=rms[i][:, j : j + 1])
 
         def scale_rows(u):
             i, j = divmod(u, TILES)
@@ -142,7 +143,7 @@ def tile_ltransformerdecoderblock_pa_t_kernel(
             nc.gpsimd.tensor_scalar(
                 out=y[u][:],
                 in0=x_sb[i][:, j, :].rearrange("r (g p t) -> r g t p", g=PASSES, t=PACK),
-                scalar1=rstd[i][:, j : j + 1], scalar2=1.0, op0=ALU.mult, op1=ALU.mult,
+                scalar1=rstd[u][:], scalar2=1.0, op0=ALU.mult, op1=ALU.mult,
             )
 
         def turn(u):
@@ -242,9 +243,10 @@ def tile_ltransformerdecoderblock_pa_t_kernel(
                 store_group((s - STORE_LAG) // TILES)
             if is_unit(s + SUM_LEAD):
                 sum_squares(s + SUM_LEAD)
-            if is_unit(s + SCALE_LEAD + 1) and (s + SCALE_LEAD + 1) % TILES == 0:
-                invert_rms((s + SCALE_LEAD + 1) // TILES)
+            if is_unit(s - QUANT_LAG):
+                quantise(s - QUANT_LAG)
             if is_unit(s + SCALE_LEAD):
+                invert_rms(s + SCALE_LEAD)
                 scale_rows(s + SCALE_LEAD)
             if is_unit(s - PROJECT_LAG):
                 project(s - PROJECT_LAG)
@@ -252,8 +254,6 @@ def tile_ltransformerdecoderblock_pa_t_kernel(
                 turn(s + TURN_LEAD)
             if is_unit(s):
                 apply_gain(s)
-            if is_unit(s - QUANT_LAG):
-                quantise(s - QUANT_LAG)
             if is_unit(s - LIFT_LAG):
                 lift(s - LIFT_LAG)
             if is_unit(s - STATS_LAG):

@@ -139,10 +139,10 @@ def tile_ltransformerdecoderblock_pa_t_kernel(
 
         def scale_rows(u):
             i, j = divmod(u, TILES)
-            y[u] = by_unit.tile([P, PASSES, PACK, P], F32, name="y")
+            y[u] = by_unit.tile([P, PACK, PASSES, P], F32, name="y")
             nc.gpsimd.tensor_scalar(
-                out=y[u][:],
-                in0=x_sb[i][:, j, :].rearrange("r (g p t) -> r g t p", g=PASSES, t=PACK),
+                out=y[u][:].rearrange("r t g (c i) -> r (g c) t i", i=4),
+                in0=x_sb[i][:, j, :].rearrange("r (c i t) -> r c t i", i=4, t=PACK),
                 scalar1=rstd[u][:], scalar2=1.0, op0=ALU.mult, op1=ALU.mult,
             )
 
@@ -150,7 +150,7 @@ def tile_ltransformerdecoderblock_pa_t_kernel(
             for g in range(PASSES):
                 turned[u, g] = psum_t.tile([P, PACK, P], F32, name="turned")
                 for t in range(PACK):
-                    nc.tensor.transpose(turned[u, g][:, t, :], y[u][:, g, t, :], ident[:])
+                    nc.tensor.transpose(turned[u, g][:, t, :], y[u][:, t, g, :], ident[:])
 
         def apply_gain(u):
             n_grouped[u] = by_unit.tile([P, PASSES, P, PACK], BF16, name="n_grouped", align_bytes=64)
@@ -243,11 +243,11 @@ def tile_ltransformerdecoderblock_pa_t_kernel(
                 store_group((s - STORE_LAG) // TILES)
             if is_unit(s + SUM_LEAD):
                 sum_squares(s + SUM_LEAD)
-            if is_unit(s - QUANT_LAG):
-                quantise(s - QUANT_LAG)
             if is_unit(s + SCALE_LEAD):
                 invert_rms(s + SCALE_LEAD)
                 scale_rows(s + SCALE_LEAD)
+            if is_unit(s - QUANT_LAG):
+                quantise(s - QUANT_LAG)
             if is_unit(s - PROJECT_LAG):
                 project(s - PROJECT_LAG)
             if is_unit(s + TURN_LEAD):

@@ -30,9 +30,11 @@ E = HEADS * HD
 OUTS = 3
 QK = 2 * E
 EPS = 1e-6
+EARLY_GROUPS = (0, 1)
+LAST_GROUPS = (GROUPS - 1,)
 
-SUM_LEAD = 8
-SCALE_LEAD = 3
+SUM_LEAD = 7
+SCALE_LEAD = 2
 TURN_LEAD = 1
 QUANT_LAG = 1
 PROJECT_LAG = 2
@@ -43,7 +45,7 @@ STORE_LAG = 6
 LOAD_AHEAD = 2
 
 
-def quantise_weights(nc, const, stage, wq, wk, wv):
+def load_weights(nc, const, stage, wq, wk, wv):
     raw = stage.tile([P, PASSES, PACK, OUTS * E], BF16)
     for o, w in enumerate((wq, wk, wv)):
         for g in range(PASSES):
@@ -51,24 +53,31 @@ def quantise_weights(nc, const, stage, wq, wk, wv):
                 out=raw[:, g, :, o * E : (o + 1) * E],
                 in_=w[g * K_PASS : (g + 1) * K_PASS, :].rearrange("(p t) n -> p t n", t=PACK),
             )
-    operands = []
+    weights = []
     for name, first, cols in (("qk", 0, QK), ("v", QK, E)):
         grouped = stage.tile([P, PASSES, cols, PACK], BF16, name="w_grouped_" + name, align_bytes=64)
+        codes = const.tile([P, PASSES, cols], U32, name="w_codes_" + name, align_bytes=64)
+        scales = const.tile([P, PASSES, cols], U8, name="w_scales_" + name, align_bytes=64)
+        weights.append((first, cols, raw, grouped, codes, scales))
+    return weights
+
+
+def group_weights(nc, weights):
+    for first, cols, raw, grouped, codes, scales in weights:
         for g in range(PASSES):
             nc.vector.tensor_copy(
                 out=grouped[:, g, :, :],
                 in_=raw[:, g, :, first : first + cols].rearrange("p t c -> p c t"),
             )
-        codes = const.tile([P, PASSES, cols], U32, name="w_codes_" + name, align_bytes=64)
-        scales = const.tile([P, PASSES, cols], U8, name="w_scales_" + name, align_bytes=64)
-        operands.append((first, cols, grouped, codes, scales))
-    for first, cols, grouped, codes, scales in operands:
+
+
+def quantise_weights(nc, weights):
+    for first, cols, raw, grouped, codes, scales in weights:
         nc.vector.quantize_mx(
             out=codes[:].rearrange("p g c -> p (g c)").bitcast(FP8X4),
             scales=scales[:].rearrange("p g c -> p (g c)"),
             in_=grouped[:].rearrange("p g c t -> p (g c t)"),
         )
-    return [(first, cols, codes, scales) for first, cols, grouped, codes, scales in operands]
 
 
 def gain_by_partition(nc, const, ln1_w):
@@ -102,6 +111,7 @@ def tile_ltransformerdecoderblock_pa_t_kernel(
         rstd = {}
         lifted = {}
         stats = {}
+        mean_sq = {}
         head_sq = {}
         y = {}
         turned = {}
@@ -110,40 +120,56 @@ def tile_ltransformerdecoderblock_pa_t_kernel(
         n_scales = {}
         product = {}
 
+        def finished_with(u, groups_by_unit):
+            i, j = divmod(u, TILES)
+            if i in groups_by_unit:
+                return slice(j, j + 1)
+            return slice(0, TILES) if j == TILES - 1 else None
+
         def load_group(i):
             x_sb[i] = x_pool.tile([P, TILES, D], BF16, name="x_sb")
-            nc.sync.dma_start(
-                out=x_sb[i][:],
-                in_=x_rows[i * GROUP : (i + 1) * GROUP, :].rearrange("(p j) d -> p j d", j=TILES),
-            )
+            rows = x_rows[i * GROUP : (i + 1) * GROUP, :].rearrange("(p j) d -> p j d", j=TILES)
+            width = 1 if i in EARLY_GROUPS else TILES
+            for j in range(0, TILES, width):
+                nc.sync.dma_start(out=x_sb[i][:, j : j + width, :], in_=rows[:, j : j + width, :])
 
         def sum_squares(u):
             i, j = divmod(u, TILES)
             if j == 0:
                 sum_sq[i] = by_group.tile([P, TILES], F32, name="sum_sq")
+                rms[i] = by_group.tile([P, TILES], F32, name="rms")
             scratch = by_unit.tile([P, D], BF16, name="scratch")
             nc.scalar.activation(
                 out=scratch[:], in_=x_sb[i][:, j, :], func=ACT.Square,
                 accum_out=sum_sq[i][:, j : j + 1],
             )
-            if j == TILES - 1:
-                rms[i] = by_group.tile([P, TILES], F32, name="rms")
+            done = finished_with(u, EARLY_GROUPS)
+            if done is not None:
                 nc.scalar.activation(
-                    out=rms[i][:], in_=sum_sq[i][:], func=ACT.Sqrt, scale=1.0 / D, bias=EPS
+                    out=rms[i][:, done], in_=sum_sq[i][:, done], func=ACT.Sqrt,
+                    scale=HD**2 / D, bias=HD**2 * EPS,
                 )
 
         def invert_rms(u):
             i, j = divmod(u, TILES)
-            rstd[u] = by_unit.tile([P, 1], F32, name="rstd")
-            nc.vector.reciprocal(out=rstd[u][:], in_=rms[i][:, j : j + 1])
+            if j == 0:
+                rstd[i] = by_group.tile([P, TILES], F32, name="rstd")
+            if i in EARLY_GROUPS:
+                nc.vector.reciprocal(out=rstd[i][:, j : j + 1], in_=rms[i][:, j : j + 1])
+            elif j == 0:
+                nc.vector.reciprocal(out=rstd[i][:], in_=rms[i][:])
 
         def scale_rows(u):
             i, j = divmod(u, TILES)
             y[u] = by_unit.tile([P, PACK, PASSES, P], F32, name="y")
+            factor = float(HD)
+            if i not in EARLY_GROUPS:
+                gi, gj = divmod(u - SCALE_LEAD - STATS_LAG - 1, TILES)
+                factor = stats[gi][:, OUTS - 1, gj, HEADS - 1, 0:1]
             nc.gpsimd.tensor_scalar(
                 out=y[u][:].rearrange("r t g (c i) -> r (g c) t i", i=4),
                 in0=x_sb[i][:, j, :].rearrange("r (c i t) -> r c t i", i=4, t=PACK),
-                scalar1=rstd[u][:], scalar2=1.0, op0=ALU.mult, op1=ALU.mult,
+                scalar1=rstd[i][:, j : j + 1], scalar2=factor, op0=ALU.mult, op1=ALU.mult,
             )
 
         def turn(u):
@@ -173,7 +199,7 @@ def tile_ltransformerdecoderblock_pa_t_kernel(
 
         def project(u):
             product[u] = psum_o.tile([P, OUTS * E], F32, name="product")
-            for first, cols, w_codes, w_scales in weights:
+            for first, cols, raw, grouped, w_codes, w_scales in weights:
                 for g in range(PASSES):
                     nc.tensor.matmul_mx(
                         out=product[u][:, first : first + cols],
@@ -202,35 +228,51 @@ def tile_ltransformerdecoderblock_pa_t_kernel(
                     in_=product[u][:, o * E : (o + 1) * E].rearrange("p (h c) -> p c h", h=HEADS),
                 )
 
-        def sum_heads(i):
-            mean_sq = by_group.tile([P, OUTS, TILES, HEADS], F32, name="mean_sq")
+        def sum_heads(u):
+            i, j = divmod(u, TILES)
+            done = finished_with(u, LAST_GROUPS)
+            if done is None:
+                return
+            if done.start == 0:
+                mean_sq[i] = by_group.tile([P, OUTS, TILES, HEADS], F32, name="mean_sq")
+                head_sq[i] = by_group.tile([P, OUTS, TILES, HEADS], F32, name="head_sq")
             nc.scalar.activation(
-                out=mean_sq[:], in_=stats[i][:, :, :, :, 1], func=ACT.Square, scale=math.sqrt(HD)
+                out=mean_sq[i][:, :, done, :], in_=stats[i][:, :, done, :, 1], func=ACT.Square,
+                scale=math.sqrt(HD),
             )
-            head_sq[i] = by_group.tile([P, OUTS, TILES, HEADS], F32, name="head_sq")
             nc.gpsimd.tensor_tensor(
-                out=head_sq[i][:], in0=stats[i][:, :, :, :, 2], in1=mean_sq[:], op=ALU.add
+                out=head_sq[i][:, :, done, :], in0=stats[i][:, :, done, :, 2],
+                in1=mean_sq[i][:, :, done, :], op=ALU.add,
             )
 
-        def store_group(i):
+        def store(u):
+            i = u // TILES
+            done = finished_with(u, LAST_GROUPS)
+            if done is None:
+                return
             nc.scalar.activation(
-                out=lifted[i][:, :, :, :, 0], in_=head_sq[i][:], func=ACT.Sqrt, bias=1.0
+                out=lifted[i][:, :, done, :, 0], in_=head_sq[i][:, :, done, :], func=ACT.Sqrt,
+                bias=1.0,
             )
             for o in range(OUTS):
+                rows = out_rows[o][i * GROUP : (i + 1) * GROUP, :]
                 nc.sync.dma_start(
-                    out=out_rows[o][i * GROUP : (i + 1) * GROUP, :].rearrange(
-                        "(p j) c -> p (j c)", j=TILES
-                    ),
-                    in_=lifted[i][:, o, :, :, :].rearrange("p j h c -> p (j h c)"),
+                    out=rows.rearrange("(p j) c -> p j c", j=TILES)[:, done, :],
+                    in_=lifted[i][:, o, done, :, :].rearrange("p j h c -> p j (h c)"),
                 )
+
+        zero = const.tile([P, 1], F32)
+        nc.vector.memset(zero[:], 0.0)
+        root = const.tile([P, 1], F32)
+        nc.scalar.activation(out=root[:], in_=zero[:], func=ACT.Sqrt)
 
         load_group(0)
         ident = const.tile([P, P], F32)
         make_identity(nc, ident[:])
         gain = gain_by_partition(nc, const, ln1_w)
-        weights = quantise_weights(nc, const, stage, wq, wk, wv)
         for i in range(1, LOAD_AHEAD):
             load_group(i)
+        weights = load_weights(nc, const, stage, wq, wk, wv)
 
         def is_unit(u):
             return 0 <= u < UNITS
@@ -239,8 +281,8 @@ def tile_ltransformerdecoderblock_pa_t_kernel(
             if is_unit(s + SUM_LEAD) and (s + SUM_LEAD) % TILES == 0:
                 if (s + SUM_LEAD) // TILES + LOAD_AHEAD < GROUPS:
                     load_group((s + SUM_LEAD) // TILES + LOAD_AHEAD)
-            if is_unit(s - STORE_LAG) and (s - STORE_LAG) % TILES == TILES - 1:
-                store_group((s - STORE_LAG) // TILES)
+            if is_unit(s - STORE_LAG):
+                store(s - STORE_LAG)
             if is_unit(s + SUM_LEAD):
                 sum_squares(s + SUM_LEAD)
             if is_unit(s + SCALE_LEAD):
@@ -254,9 +296,13 @@ def tile_ltransformerdecoderblock_pa_t_kernel(
                 turn(s + TURN_LEAD)
             if is_unit(s):
                 apply_gain(s)
+            if s == 0:
+                group_weights(nc, weights)
+            if s == 1:
+                quantise_weights(nc, weights)
             if is_unit(s - LIFT_LAG):
                 lift(s - LIFT_LAG)
             if is_unit(s - STATS_LAG):
                 head_stats(s - STATS_LAG)
-            if is_unit(s - SUM_LAG) and (s - SUM_LAG) % TILES == TILES - 1:
-                sum_heads((s - SUM_LAG) // TILES)
+            if is_unit(s - SUM_LAG):
+                sum_heads(s - SUM_LAG)

@@ -102,7 +102,8 @@ def tile_ltransformerdecoderblock_pa_t_kernel(
         by_group = ctx.enter_context(tc.tile_pool(name="by_group", bufs=4))
         by_unit = ctx.enter_context(tc.tile_pool(name="by_unit", bufs=4))
         psum_t = ctx.enter_context(tc.psum_pool(name="psum_t", bufs=4))
-        psum_o = ctx.enter_context(tc.psum_pool(name="psum_o", bufs=4))
+        psum_o = ctx.enter_context(tc.psum_pool(name="psum_o", bufs=3))
+        psum_w = ctx.enter_context(tc.psum_pool(name="psum_w", bufs=1))
         ctx.enter_context(tc.manual_schedule())
 
         x_sb = {}
@@ -211,6 +212,20 @@ def tile_ltransformerdecoderblock_pa_t_kernel(
                         stop=(g == PASSES - 1),
                     )
 
+        def keep_clock_up(u):
+            idle = psum_w.tile([P, QK], F32, name="idle")
+            first, cols, raw, grouped, w_codes, w_scales = weights[0]
+            for g in range(PASSES):
+                nc.tensor.matmul_mx(
+                    out=idle[:],
+                    lhsT=n_codes[u][:, g, :].bitcast(FP8X4),
+                    lhsT_scale=n_scales[u][:, g, :],
+                    rhs=w_codes[:, g, :].bitcast(FP8X4),
+                    rhs_scale=w_scales[:, g, :],
+                    start=True,
+                    stop=True,
+                )
+
         def lift(u):
             i, j = divmod(u, TILES)
             if j == 0:
@@ -294,6 +309,8 @@ def tile_ltransformerdecoderblock_pa_t_kernel(
                 project(s - PROJECT_LAG)
             if is_unit(s + TURN_LEAD):
                 turn(s + TURN_LEAD)
+            if is_unit(s - PROJECT_LAG):
+                keep_clock_up(s - PROJECT_LAG)
             if is_unit(s):
                 apply_gain(s)
             if s == 0:

@@ -31,7 +31,7 @@ OUTS = 3
 QK = 2 * E
 EPS = 1e-6
 EARLY_GROUPS = (0, 1)
-LAST_GROUPS = (GROUPS - 1,)
+LAST_GROUPS = (GROUPS - 2, GROUPS - 1)
 
 SUM_LEAD = 7
 SCALE_LEAD = 2
@@ -42,6 +42,7 @@ LIFT_LAG = 3
 STATS_LAG = 4
 SUM_LAG = 5
 STORE_LAG = 6
+LAST_STORE_LAG = 4
 LOAD_AHEAD = 2
 
 
@@ -112,7 +113,6 @@ def tile_ltransformerdecoderblock_pa_t_kernel(
         rstd = {}
         lifted = {}
         stats = {}
-        mean_sq = {}
         head_sq = {}
         y = {}
         turned = {}
@@ -148,29 +148,21 @@ def tile_ltransformerdecoderblock_pa_t_kernel(
             if done is not None:
                 nc.scalar.activation(
                     out=rms[i][:, done], in_=sum_sq[i][:, done], func=ACT.Sqrt,
-                    scale=HD**2 / D, bias=HD**2 * EPS,
+                    scale=1.0 / D, bias=EPS,
                 )
 
         def invert_rms(u):
             i, j = divmod(u, TILES)
-            if j == 0:
-                rstd[i] = by_group.tile([P, TILES], F32, name="rstd")
-            if i in EARLY_GROUPS:
-                nc.vector.reciprocal(out=rstd[i][:, j : j + 1], in_=rms[i][:, j : j + 1])
-            elif j == 0:
-                nc.vector.reciprocal(out=rstd[i][:], in_=rms[i][:])
+            rstd[u] = by_unit.tile([P, 1], F32, name="rstd")
+            nc.vector.reciprocal(out=rstd[u][:], in_=rms[i][:, j : j + 1])
 
         def scale_rows(u):
             i, j = divmod(u, TILES)
             y[u] = by_unit.tile([P, PACK, PASSES, P], F32, name="y")
-            factor = float(HD)
-            if i not in EARLY_GROUPS:
-                gi, gj = divmod(u - SCALE_LEAD - STATS_LAG - 1, TILES)
-                factor = stats[gi][:, OUTS - 1, gj, HEADS - 1, 0:1]
             nc.gpsimd.tensor_scalar(
                 out=y[u][:].rearrange("r t g (c i) -> r (g c) t i", i=4),
                 in0=x_sb[i][:, j, :].rearrange("r (c i t) -> r c t i", i=4, t=PACK),
-                scalar1=rstd[i][:, j : j + 1], scalar2=factor, op0=ALU.mult, op1=ALU.mult,
+                scalar1=rstd[u][:], scalar2=0.0, op0=ALU.mult, op1=ALU.add,
             )
 
         def turn(u):
@@ -230,8 +222,20 @@ def tile_ltransformerdecoderblock_pa_t_kernel(
             i, j = divmod(u, TILES)
             if j == 0:
                 lifted[i] = by_group.tile([P, OUTS, TILES, HEADS, 1 + HD], F32, name="lifted")
+                head_sq[i] = by_group.tile([P, OUTS, TILES, HEADS], F32, name="head_sq")
             by_head = product[u][:].rearrange("p (o h c) -> p o h c", o=OUTS, h=HEADS)
             nc.scalar.copy(out=lifted[i][:, :, j, :, 1:], in_=by_head)
+
+        def head_squares(u):
+            i, j = divmod(u, TILES)
+            for o in range(OUTS):
+                for h in range(HEADS):
+                    first = o * E + h * HD
+                    square = by_unit.tile([P, HD], F32, name="square")
+                    nc.scalar.activation(
+                        out=square[:], in_=product[u][:, first : first + HD], func=ACT.Square,
+                        accum_out=head_sq[i][:, o, j, h : h + 1],
+                    )
 
         def head_stats(u):
             i, j = divmod(u, TILES)
@@ -243,21 +247,13 @@ def tile_ltransformerdecoderblock_pa_t_kernel(
                     in_=product[u][:, o * E : (o + 1) * E].rearrange("p (h c) -> p c h", h=HEADS),
                 )
 
-        def sum_heads(u):
-            i, j = divmod(u, TILES)
-            done = finished_with(u, LAST_GROUPS)
-            if done is None:
-                return
-            if done.start == 0:
-                mean_sq[i] = by_group.tile([P, OUTS, TILES, HEADS], F32, name="mean_sq")
-                head_sq[i] = by_group.tile([P, OUTS, TILES, HEADS], F32, name="head_sq")
+        def sum_heads(i):
+            mean_sq = by_group.tile([P, OUTS, TILES, HEADS], F32, name="mean_sq")
             nc.scalar.activation(
-                out=mean_sq[i][:, :, done, :], in_=stats[i][:, :, done, :, 1], func=ACT.Square,
-                scale=math.sqrt(HD),
+                out=mean_sq[:], in_=stats[i][:, :, :, :, 1], func=ACT.Square, scale=math.sqrt(HD)
             )
             nc.gpsimd.tensor_tensor(
-                out=head_sq[i][:, :, done, :], in0=stats[i][:, :, done, :, 2],
-                in1=mean_sq[i][:, :, done, :], op=ALU.add,
+                out=head_sq[i][:], in0=stats[i][:, :, :, :, 2], in1=mean_sq[:], op=ALU.add
             )
 
         def store(u):
@@ -292,12 +288,17 @@ def tile_ltransformerdecoderblock_pa_t_kernel(
         def is_unit(u):
             return 0 <= u < UNITS
 
+        def is_last(u):
+            return is_unit(u) and u // TILES in LAST_GROUPS
+
         for s in range(-SUM_LEAD, UNITS + STORE_LAG):
             if is_unit(s + SUM_LEAD) and (s + SUM_LEAD) % TILES == 0:
                 if (s + SUM_LEAD) // TILES + LOAD_AHEAD < GROUPS:
                     load_group((s + SUM_LEAD) // TILES + LOAD_AHEAD)
-            if is_unit(s - STORE_LAG):
+            if is_unit(s - STORE_LAG) and not is_last(s - STORE_LAG):
                 store(s - STORE_LAG)
+            if is_last(s - LAST_STORE_LAG):
+                store(s - LAST_STORE_LAG)
             if is_unit(s + SUM_LEAD):
                 sum_squares(s + SUM_LEAD)
             if is_unit(s + SCALE_LEAD):
@@ -319,7 +320,10 @@ def tile_ltransformerdecoderblock_pa_t_kernel(
                 quantise_weights(nc, weights)
             if is_unit(s - LIFT_LAG):
                 lift(s - LIFT_LAG)
-            if is_unit(s - STATS_LAG):
+            if is_last(s - LIFT_LAG):
+                head_squares(s - LIFT_LAG)
+            if is_unit(s - STATS_LAG) and not is_last(s - STATS_LAG):
                 head_stats(s - STATS_LAG)
-            if is_unit(s - SUM_LAG):
-                sum_heads(s - SUM_LAG)
+            if is_unit(s - SUM_LAG) and not is_last(s - SUM_LAG):
+                if (s - SUM_LAG) % TILES == TILES - 1:
+                    sum_heads((s - SUM_LAG) // TILES)

import math
from contextlib import ExitStack

import concourse.mybir as mybir
from concourse.masks import make_identity

FLOPS = 2 * 4 * 2048 * 1024 * 384

F32 = mybir.dt.float32
BF16 = mybir.dt.bfloat16
U32 = mybir.dt.uint32
U8 = mybir.dt.uint8
FP8X4 = mybir.dt.float8_e4m3fn_x4
ACT = mybir.ActivationFunctionType
ALU = mybir.AluOpType

P = 128
PACK = 4
K_PASS = P * PACK
D = 1024
PASSES = D // K_PASS
TOKENS = 4 * 2048
TILES = 4
GROUP = TILES * P
GROUPS = TOKENS // GROUP
UNITS = GROUPS * TILES
HEADS = 2
HD = 64
E = HEADS * HD
OUTS = 3
QK = 2 * E
EPS = 1e-6
EARLY_GROUPS = (0, 1)
LAST_GROUPS = (GROUPS - 2, GROUPS - 1)

SUM_LEAD = 7
SCALE_LEAD = 2
TURN_LEAD = 1
QUANT_LAG = 1
PROJECT_LAG = 2
LIFT_LAG = 3
STATS_LAG = 4
SUM_LAG = 5
STORE_LAG = 6
LAST_STORE_LAG = 4
LOAD_AHEAD = 2


def load_weights(nc, const, stage, wq, wk, wv):
    raw = stage.tile([P, PASSES, PACK, OUTS * E], BF16)
    for o, w in enumerate((wq, wk, wv)):
        for g in range(PASSES):
            nc.sync.dma_start(
                out=raw[:, g, :, o * E : (o + 1) * E],
                in_=w[g * K_PASS : (g + 1) * K_PASS, :].rearrange("(p t) n -> p t n", t=PACK),
            )
    weights = []
    for name, first, cols in (("qk", 0, QK), ("v", QK, E)):
        grouped = stage.tile([P, PASSES, cols, PACK], BF16, name="w_grouped_" + name, align_bytes=64)
        codes = const.tile([P, PASSES, cols], U32, name="w_codes_" + name, align_bytes=64)
        scales = const.tile([P, PASSES, cols], U8, name="w_scales_" + name, align_bytes=64)
        weights.append((first, cols, raw, grouped, codes, scales))
    return weights


def group_weights(nc, weights):
    for first, cols, raw, grouped, codes, scales in weights:
        for g in range(PASSES):
            nc.vector.tensor_copy(
                out=grouped[:, g, :, :],
                in_=raw[:, g, :, first : first + cols].rearrange("p t c -> p c t"),
            )


def quantise_weights(nc, weights):
    for first, cols, raw, grouped, codes, scales in weights:
        nc.vector.quantize_mx(
            out=codes[:].rearrange("p g c -> p (g c)").bitcast(FP8X4),
            scales=scales[:].rearrange("p g c -> p (g c)"),
            in_=grouped[:].rearrange("p g c t -> p (g c t)"),
        )


def gain_by_partition(nc, const, ln1_w):
    raw = const.tile([P, PASSES, PACK], BF16, name="gain_raw")
    nc.sync.dma_start(out=raw[:], in_=ln1_w.rearrange("(g p t) -> p g t", g=PASSES, t=PACK))
    gain = const.tile([P, PASSES, PACK], F32)
    nc.vector.tensor_copy(out=gain[:], in_=raw[:])
    return gain


def tile_ltransformerdecoderblock_pa_t_kernel(
    tc, x_space, ln1_w, wq, wk, wv, out_0, out_1, out_2
):
    nc = tc.nc
    x_rows = x_space.rearrange("b s d -> (b s) d")
    out_rows = [o.rearrange("b s h c -> (b s) (h c)") for o in (out_0, out_1, out_2)]

    with ExitStack() as ctx:
        const = ctx.enter_context(tc.tile_pool(name="const", bufs=1))
        stage = ctx.enter_context(tc.tile_pool(name="stage", bufs=1))
        x_pool = ctx.enter_context(tc.tile_pool(name="x", bufs=LOAD_AHEAD + 3))
        by_group = ctx.enter_context(tc.tile_pool(name="by_group", bufs=4))
        by_unit = ctx.enter_context(tc.tile_pool(name="by_unit", bufs=4))
        psum_t = ctx.enter_context(tc.psum_pool(name="psum_t", bufs=4))
        psum_o = ctx.enter_context(tc.psum_pool(name="psum_o", bufs=3))
        psum_w = ctx.enter_context(tc.psum_pool(name="psum_w", bufs=1))
        ctx.enter_context(tc.manual_schedule())

        x_sb = {}
        sum_sq = {}
        rms = {}
        rstd = {}
        lifted = {}
        stats = {}
        head_sq = {}
        y = {}
        turned = {}
        n_grouped = {}
        n_codes = {}
        n_scales = {}
        product = {}

        def finished_with(u, groups_by_unit):
            i, j = divmod(u, TILES)
            if i in groups_by_unit:
                return slice(j, j + 1)
            return slice(0, TILES) if j == TILES - 1 else None

        def load_group(i):
            x_sb[i] = x_pool.tile([P, TILES, D], BF16, name="x_sb")
            rows = x_rows[i * GROUP : (i + 1) * GROUP, :].rearrange("(p j) d -> p j d", j=TILES)
            width = 1 if i in EARLY_GROUPS else TILES
            for j in range(0, TILES, width):
                nc.sync.dma_start(out=x_sb[i][:, j : j + width, :], in_=rows[:, j : j + width, :])

        def sum_squares(u):
            i, j = divmod(u, TILES)
            if j == 0:
                sum_sq[i] = by_group.tile([P, TILES], F32, name="sum_sq")
                rms[i] = by_group.tile([P, TILES], F32, name="rms")
            scratch = by_unit.tile([P, D], BF16, name="scratch")
            nc.scalar.activation(
                out=scratch[:], in_=x_sb[i][:, j, :], func=ACT.Square,
                accum_out=sum_sq[i][:, j : j + 1],
            )
            done = finished_with(u, EARLY_GROUPS)
            if done is not None:
                nc.scalar.activation(
                    out=rms[i][:, done], in_=sum_sq[i][:, done], func=ACT.Sqrt,
                    scale=1.0 / D, bias=EPS,
                )

        def invert_rms(u):
            i, j = divmod(u, TILES)
            rstd[u] = by_unit.tile([P, 1], F32, name="rstd")
            nc.vector.reciprocal(out=rstd[u][:], in_=rms[i][:, j : j + 1])

        def scale_rows(u):
            i, j = divmod(u, TILES)
            y[u] = by_unit.tile([P, PACK, PASSES, P], F32, name="y")
            nc.gpsimd.tensor_scalar(
                out=y[u][:].rearrange("r t g (c i) -> r (g c) t i", i=4),
                in0=x_sb[i][:, j, :].rearrange("r (c i t) -> r c t i", i=4, t=PACK),
                scalar1=rstd[u][:], scalar2=0.0, op0=ALU.mult, op1=ALU.add,
            )

        def turn(u):
            for g in range(PASSES):
                turned[u, g] = psum_t.tile([P, PACK, P], F32, name="turned")
                for t in range(PACK):
                    nc.tensor.transpose(turned[u, g][:, t, :], y[u][:, t, g, :], ident[:])

        def apply_gain(u):
            n_grouped[u] = by_unit.tile([P, PASSES, P, PACK], BF16, name="n_grouped", align_bytes=64)
            for g in range(PASSES):
                nc.vector.tensor_tensor(
                    out=n_grouped[u][:, g, :, :],
                    in0=turned[u, g][:].rearrange("p t r -> p r t"),
                    in1=gain[:, g, :].unsqueeze(1).to_broadcast([P, P, PACK]),
                    op=ALU.mult,
                )

        def quantise(u):
            n_codes[u] = by_unit.tile([P, PASSES, P], U32, name="n_codes", align_bytes=64)
            n_scales[u] = by_unit.tile([P, PASSES, P], U8, name="n_scales", align_bytes=64)
            nc.vector.quantize_mx(
                out=n_codes[u][:].rearrange("p g r -> p (g r)").bitcast(FP8X4),
                scales=n_scales[u][:].rearrange("p g r -> p (g r)"),
                in_=n_grouped[u][:].rearrange("p g r t -> p (g r t)"),
            )

        def project(u):
            product[u] = psum_o.tile([P, OUTS * E], F32, name="product")
            for first, cols, raw, grouped, w_codes, w_scales in weights:
                for g in range(PASSES):
                    nc.tensor.matmul_mx(
                        out=product[u][:, first : first + cols],
                        lhsT=n_codes[u][:, g, :].bitcast(FP8X4),
                        lhsT_scale=n_scales[u][:, g, :],
                        rhs=w_codes[:, g, :].bitcast(FP8X4),
                        rhs_scale=w_scales[:, g, :],
                        start=(g == 0),
                        stop=(g == PASSES - 1),
                    )

        def keep_clock_up(u):
            idle = psum_w.tile([P, QK], F32, name="idle")
            first, cols, raw, grouped, w_codes, w_scales = weights[0]
            for g in range(PASSES):
                nc.tensor.matmul_mx(
                    out=idle[:],
                    lhsT=n_codes[u][:, g, :].bitcast(FP8X4),
                    lhsT_scale=n_scales[u][:, g, :],
                    rhs=w_codes[:, g, :].bitcast(FP8X4),
                    rhs_scale=w_scales[:, g, :],
                    start=True,
                    stop=True,
                )

        def lift(u):
            i, j = divmod(u, TILES)
            if j == 0:
                lifted[i] = by_group.tile([P, OUTS, TILES, HEADS, 1 + HD], F32, name="lifted")
                head_sq[i] = by_group.tile([P, OUTS, TILES, HEADS], F32, name="head_sq")
            by_head = product[u][:].rearrange("p (o h c) -> p o h c", o=OUTS, h=HEADS)
            nc.scalar.copy(out=lifted[i][:, :, j, :, 1:], in_=by_head)

        def head_squares(u):
            i, j = divmod(u, TILES)
            for o in range(OUTS):
                for h in range(HEADS):
                    first = o * E + h * HD
                    square = by_unit.tile([P, HD], F32, name="square")
                    nc.scalar.activation(
                        out=square[:], in_=product[u][:, first : first + HD], func=ACT.Square,
                        accum_out=head_sq[i][:, o, j, h : h + 1],
                    )

        def head_stats(u):
            i, j = divmod(u, TILES)
            if j == 0:
                stats[i] = by_group.tile([P, OUTS, TILES, HEADS, 3], F32, name="stats")
            for o in range(OUTS):
                nc.vector.bn_stats(
                    out=stats[i][:, o, j, :, :].rearrange("p h m -> p (h m)"),
                    in_=product[u][:, o * E : (o + 1) * E].rearrange("p (h c) -> p c h", h=HEADS),
                )

        def sum_heads(i):
            mean_sq = by_group.tile([P, OUTS, TILES, HEADS], F32, name="mean_sq")
            nc.scalar.activation(
                out=mean_sq[:], in_=stats[i][:, :, :, :, 1], func=ACT.Square, scale=math.sqrt(HD)
            )
            nc.gpsimd.tensor_tensor(
                out=head_sq[i][:], in0=stats[i][:, :, :, :, 2], in1=mean_sq[:], op=ALU.add
            )

        def store(u):
            i = u // TILES
            done = finished_with(u, LAST_GROUPS)
            if done is None:
                return
            nc.scalar.activation(
                out=lifted[i][:, :, done, :, 0], in_=head_sq[i][:, :, done, :], func=ACT.Sqrt,
                bias=1.0,
            )
            for o in range(OUTS):
                rows = out_rows[o][i * GROUP : (i + 1) * GROUP, :]
                nc.sync.dma_start(
                    out=rows.rearrange("(p j) c -> p j c", j=TILES)[:, done, :],
                    in_=lifted[i][:, o, done, :, :].rearrange("p j h c -> p j (h c)"),
                )

        zero = const.tile([P, 1], F32)
        nc.vector.memset(zero[:], 0.0)
        root = const.tile([P, 1], F32)
        nc.scalar.activation(out=root[:], in_=zero[:], func=ACT.Sqrt)

        load_group(0)
        ident = const.tile([P, P], F32)
        make_identity(nc, ident[:])
        gain = gain_by_partition(nc, const, ln1_w)
        for i in range(1, LOAD_AHEAD):
            load_group(i)
        weights = load_weights(nc, const, stage, wq, wk, wv)

        def is_unit(u):
            return 0 <= u < UNITS

        def is_last(u):
            return is_unit(u) and u // TILES in LAST_GROUPS

        for s in range(-SUM_LEAD, UNITS + STORE_LAG):
            if is_unit(s + SUM_LEAD) and (s + SUM_LEAD) % TILES == 0:
                if (s + SUM_LEAD) // TILES + LOAD_AHEAD < GROUPS:
                    load_group((s + SUM_LEAD) // TILES + LOAD_AHEAD)
            if is_unit(s - STORE_LAG) and not is_last(s - STORE_LAG):
                store(s - STORE_LAG)
            if is_last(s - LAST_STORE_LAG):
                store(s - LAST_STORE_LAG)
            if is_unit(s + SUM_LEAD):
                sum_squares(s + SUM_LEAD)
            if is_unit(s + SCALE_LEAD):
                invert_rms(s + SCALE_LEAD)
                scale_rows(s + SCALE_LEAD)
            if is_unit(s - QUANT_LAG):
                quantise(s - QUANT_LAG)
            if is_unit(s - PROJECT_LAG):
                project(s - PROJECT_LAG)
            if is_unit(s + TURN_LEAD):
                turn(s + TURN_LEAD)
            if is_unit(s - PROJECT_LAG):
                keep_clock_up(s - PROJECT_LAG)
            if is_unit(s):
                apply_gain(s)
            if s == 0:
                group_weights(nc, weights)
            if s == 1:
                quantise_weights(nc, weights)
            if is_unit(s - LIFT_LAG):
                lift(s - LIFT_LAG)
            if is_last(s - LIFT_LAG):
                head_squares(s - LIFT_LAG)
            if is_unit(s - STATS_LAG) and not is_last(s - STATS_LAG):
                head_stats(s - STATS_LAG)
            if is_unit(s - SUM_LAG) and not is_last(s - SUM_LAG):
                if (s - SUM_LAG) % TILES == TILES - 1:
                    sum_heads((s - SUM_LAG) // TILES)
